import numpy as np
import ml_dtypes

BF16 = ml_dtypes.bfloat16


def bf(x):
    return np.asarray(x, np.float32).astype(BF16)


def f32(x):
    return np.asarray(x, np.float32)


def f64(x):
    return np.asarray(x).astype(np.float64)


def striped(idx):
    return np.tile(idx.reshape(-1, 16).T, (8, 1))


C, H, S, N, K = 256, 128, 512, 256, 3
W2_SCALE, B1_SCALE = 3.0, 0.5


def sigmoid(v):
    return 1.0 / (1.0 + np.exp(-v))


def setup_inputs():
    r = np.random.standard_normal((H, 1))
    return {
        "base": f32(np.random.standard_normal((C, S))),
        "xs": f32(np.random.standard_normal((C, N))),
        "vals": f32(np.random.standard_normal((C, N))),
        "xo": f32(np.random.standard_normal((C, N))),
        "w1": bf(np.random.standard_normal((C, H)) / np.sqrt(C)),
        "b1": f32(B1_SCALE * np.random.standard_normal((H, 1))),
        "w2": bf(W2_SCALE * (r - r.mean()) / np.sqrt(H)),
        "offs": striped(np.random.permutation(S)[:N]),
    }


def reference(base, xs, vals, xo, w1, b1, w2, offs):
    idx = offs[:16].T.reshape(-1)
    feats = np.concatenate([f64(xs), f64(vals), f64(xo)], axis=1)
    hid = np.maximum(f64(w1).T @ feats + f64(b1), 0.0)
    s = sigmoid((f64(w2) * hid).sum(axis=0)).reshape(K, N)
    e = np.exp(s)
    share = e[1] / e.sum(axis=0)
    out = f64(base).copy()
    out[:, idx] = f64(vals) * share[None, :]
    return out

@@ -1,0 +1,84 @@
+import concourse.mybir as mybir
+
+F32 = mybir.dt.float32
+BF16 = mybir.dt.bfloat16
+U16 = mybir.dt.uint16
+ALU = mybir.AluOpType
+ACT = mybir.ActivationFunctionType
+
+P = 128
+C, H, S, N = 256, 128, 512, 256
+CB = C // P
+VIEWS = 3
+VALS = 1
+
+FLOPS = 2 * C * H * VIEWS * N + 2 * H * VIEWS * N
+
+
+def tile_attentionnetwork_kernel(tc, base, xs, vals, xo, w1, b1, w2, offs, out):
+    nc = tc.nc
+    base_blocks = base.rearrange("(cb p) s -> cb p s", p=P)
+    out_blocks = out.rearrange("(cb p) s -> cb p s", p=P)
+
+    with (
+        tc.tile_pool(name="held", bufs=1) as held,
+        tc.psum_pool(name="psum", bufs=1) as psum,
+    ):
+        w1_sb = held.tile([P, CB, H], BF16, name="w1_sb")
+        nc.scalar.dma_start(w1_sb[:], w1.rearrange("(cb p) h -> p cb h", p=P))
+        view_f32 = []
+        for u, (view, queue) in enumerate(((xs, nc.sync), (vals, nc.scalar), (xo, nc.sync))):
+            loaded = held.tile([P, CB, N], F32, name=f"view_f32_{u}")
+            queue.dma_start(loaded[:], view.rearrange("(cb p) n -> p cb n", p=P))
+            view_f32.append(loaded)
+        b1_sb = held.tile([P, 1], F32, name="b1_sb")
+        nc.gpsimd.dma_start(b1_sb[:], b1)
+        w2_sb = held.tile([P, 1], BF16, name="w2_sb")
+        nc.gpsimd.dma_start(w2_sb[:], w2)
+        offsets = held.tile([P, N // 16], U16, name="offsets")
+        nc.sync.dma_start(offsets[:], offs)
+        windows = []
+        for cb, queue in enumerate((nc.sync, nc.scalar)):
+            window = held.tile([P, S], F32, name=f"window_{cb}")
+            queue.dma_start(window[:], base_blocks[cb])
+            windows.append(window)
+
+        warm = held.tile([P, 1], F32, name="warm")
+        nc.vector.memset(warm[:], 0.0)
+        nc.scalar.activation(warm[:], warm[:], ACT.Exp)
+
+        w2_rep = held.tile([P, P], BF16, name="w2_rep")
+        nc.vector.tensor_copy(w2_rep[:], w2_sb[:, 0:1].to_broadcast([P, P]))
+
+        expd = []
+        for u in range(VIEWS):
+            view_bf = held.tile([P, CB, N], BF16, name=f"view_bf_{u}")
+            nc.vector.tensor_copy(view_bf[:], view_f32[u][:])
+            hid_ps = psum.tile([P, N], F32, name=f"hid_ps_{u}")
+            for cb in range(CB):
+                nc.tensor.matmul(
+                    hid_ps[:], w1_sb[:, cb, :], view_bf[:, cb, :], start=(cb == 0), stop=(cb == CB - 1)
+                )
+            hid_bf = held.tile([P, N], BF16, name=f"hid_bf_{u}")
+            nc.scalar.activation(hid_bf[:], hid_ps[:], ACT.Relu, bias=b1_sb[:, 0:1])
+            score_ps = psum.tile([P, N], F32, name=f"score_ps_{u}")
+            nc.tensor.matmul(score_ps[:], w2_rep[:], hid_bf[:], start=True, stop=True)
+            tanh_u = held.tile([P, N], F32, name=f"tanh_{u}")
+            nc.scalar.activation(tanh_u[:], score_ps[:], ACT.Tanh, scale=0.5)
+            exp_u = held.tile([P, N], F32, name=f"exp_{u}")
+            nc.scalar.activation(exp_u[:], tanh_u[:], ACT.Exp, scale=0.5)
+            expd.append(exp_u)
+
+        total = held.tile([P, N], F32, name="total")
+        nc.vector.tensor_tensor(total[:], expd[0][:], expd[1][:], ALU.add)
+        nc.vector.tensor_tensor(total[:], total[:], expd[2][:], ALU.add)
+        inverse = held.tile([P, N], F32, name="inverse")
+        nc.vector.reciprocal(inverse[:], total[:])
+        share = held.tile([P, N], F32, name="share")
+        nc.vector.tensor_tensor(share[:], expd[VALS][:], inverse[:], ALU.mult)
+
+        for cb, queue in enumerate((nc.sync, nc.scalar)):
+            nc.vector.tensor_tensor(
+                windows[cb][:].indirect(offsets[:]), view_f32[VALS][:, cb, :], share[:], ALU.mult
+            )
+            queue.dma_start(out_blocks[cb], windows[cb][:])

@@ -1,4 +1,5 @@
 import concourse.mybir as mybir
+from concourse.masks import make_identity
 
 F32 = mybir.dt.float32
 BF16 = mybir.dt.bfloat16
@@ -9,6 +10,7 @@ ACT = mybir.ActivationFunctionType
 P = 128
 C, H, S, N = 256, 128, 512, 256
 CB = C // P
+JB = N // P
 VIEWS = 3
 VALS = 1
 
@@ -24,6 +26,10 @@ def tile_attentionnetwork_kernel(tc, base, xs, vals, xo, w1, b1, w2, offs, out):
         tc.tile_pool(name="held", bufs=1) as held,
         tc.psum_pool(name="psum", bufs=1) as psum,
     ):
+        b1_sb = held.tile([P, 1], F32, name="b1_sb")
+        nc.sync.dma_start(b1_sb[:], b1)
+        w2_sb = held.tile([P, 1], BF16, name="w2_sb")
+        nc.scalar.dma_start(w2_sb[:], w2)
         w1_sb = held.tile([P, CB, H], BF16, name="w1_sb")
         nc.scalar.dma_start(w1_sb[:], w1.rearrange("(cb p) h -> p cb h", p=P))
         view_f32 = []
@@ -31,10 +37,6 @@ def tile_attentionnetwork_kernel(tc, base, xs, vals, xo, w1, b1, w2, offs, out):
             loaded = held.tile([P, CB, N], F32, name=f"view_f32_{u}")
             queue.dma_start(loaded[:], view.rearrange("(cb p) n -> p cb n", p=P))
             view_f32.append(loaded)
-        b1_sb = held.tile([P, 1], F32, name="b1_sb")
-        nc.gpsimd.dma_start(b1_sb[:], b1)
-        w2_sb = held.tile([P, 1], BF16, name="w2_sb")
-        nc.gpsimd.dma_start(w2_sb[:], w2)
         offsets = held.tile([P, N // 16], U16, name="offsets")
         nc.sync.dma_start(offsets[:], offs)
         windows = []
@@ -43,14 +45,12 @@ def tile_attentionnetwork_kernel(tc, base, xs, vals, xo, w1, b1, w2, offs, out):
             queue.dma_start(window[:], base_blocks[cb])
             windows.append(window)
 
-        warm = held.tile([P, 1], F32, name="warm")
-        nc.vector.memset(warm[:], 0.0)
-        nc.scalar.activation(warm[:], warm[:], ACT.Exp)
+        identity = held.tile([P, P], F32, name="identity")
+        make_identity(nc, identity[:])
+        ones = held.tile([P, P], F32, name="ones")
+        nc.gpsimd.memset(ones[:], 1.0)
 
-        w2_rep = held.tile([P, P], BF16, name="w2_rep")
-        nc.vector.tensor_copy(w2_rep[:], w2_sb[:, 0:1].to_broadcast([P, P]))
-
-        expd = []
+        score_ps = psum.tile([P, JB, VIEWS], F32, name="score_ps")
         for u in range(VIEWS):
             view_bf = held.tile([P, CB, N], BF16, name=f"view_bf_{u}")
             nc.vector.tensor_copy(view_bf[:], view_f32[u][:])
@@ -61,21 +61,34 @@ def tile_attentionnetwork_kernel(tc, base, xs, vals, xo, w1, b1, w2, offs, out):
                 )
             hid_bf = held.tile([P, N], BF16, name=f"hid_bf_{u}")
             nc.scalar.activation(hid_bf[:], hid_ps[:], ACT.Relu, bias=b1_sb[:, 0:1])
-            score_ps = psum.tile([P, N], F32, name=f"score_ps_{u}")
-            nc.tensor.matmul(score_ps[:], w2_rep[:], hid_bf[:], start=True, stop=True)
-            tanh_u = held.tile([P, N], F32, name=f"tanh_{u}")
-            nc.scalar.activation(tanh_u[:], score_ps[:], ACT.Tanh, scale=0.5)
-            exp_u = held.tile([P, N], F32, name=f"exp_{u}")
-            nc.scalar.activation(exp_u[:], tanh_u[:], ACT.Exp, scale=0.5)
-            expd.append(exp_u)
+            for jb in range(JB):
+                nc.tensor.matmul(
+                    score_ps[:, jb, u : u + 1], hid_bf[:, jb * P : (jb + 1) * P], w2_sb[:], start=True, stop=True
+                )
 
-        total = held.tile([P, N], F32, name="total")
-        nc.vector.tensor_tensor(total[:], expd[0][:], expd[1][:], ALU.add)
-        nc.vector.tensor_tensor(total[:], total[:], expd[2][:], ALU.add)
-        inverse = held.tile([P, N], F32, name="inverse")
+        tanhs = held.tile([P, JB, VIEWS], F32, name="tanhs")
+        nc.scalar.activation(tanhs[:], score_ps[:], ACT.Tanh, scale=0.5)
+        exps = held.tile([P, JB, VIEWS], F32, name="exps")
+        nc.scalar.activation(exps[:], tanhs[:], ACT.Exp, scale=0.5)
+        total = held.tile([P, JB], F32, name="total")
+        nc.vector.tensor_reduce(total[:], exps[:], mybir.AxisListType.X, ALU.add)
+        inverse = held.tile([P, JB], F32, name="inverse")
         nc.vector.reciprocal(inverse[:], total[:])
+
+        share_cols = held.tile([P, JB, P], F32, name="share_cols")
+        share_ps = psum.tile([P, JB, P], F32, name="share_ps")
+        for jb in range(JB):
+            nc.vector.tensor_scalar(
+                share_cols[:, jb, :],
+                ones[:],
+                exps[:, jb, VALS : VALS + 1],
+                inverse[:, jb : jb + 1],
+                ALU.mult,
+                ALU.mult,
+            )
+            nc.tensor.transpose(share_ps[:, jb, :], share_cols[:, jb, :], identity[:])
         share = held.tile([P, N], F32, name="share")
-        nc.vector.tensor_tensor(share[:], expd[VALS][:], inverse[:], ALU.mult)
+        nc.vector.tensor_copy(share[:], share_ps[:].rearrange("p jb j -> p (jb j)"))
 
         for cb, queue in enumerate((nc.sync, nc.scalar)):
             nc.vector.tensor_tensor(

@@ -13,6 +13,7 @@ CB = C // P
 JB = N // P
 VIEWS = 3
 VALS = 1
+OFFS_COLS = P // 16
 
 FLOPS = 2 * C * H * VIEWS * N + 2 * H * VIEWS * N
 
@@ -21,77 +22,90 @@ def tile_attentionnetwork_kernel(tc, base, xs, vals, xo, w1, b1, w2, offs, out):
     nc = tc.nc
     base_blocks = base.rearrange("(cb p) s -> cb p s", p=P)
     out_blocks = out.rearrange("(cb p) s -> cb p s", p=P)
+    hw_queues = (nc.sync, nc.scalar)
 
     with (
         tc.tile_pool(name="held", bufs=1) as held,
         tc.psum_pool(name="psum", bufs=1) as psum,
     ):
+        view_f32 = {}
+
+        def load_views(jb):
+            for u, view in enumerate((xs, vals, xo)):
+                loaded = held.tile([P, CB, P], F32, name=f"view_f32_{jb}_{u}")
+                hw_queues[(jb * VIEWS + u) % 2].dma_start(
+                    loaded[:], view[:, jb * P : (jb + 1) * P].rearrange("(cb p) j -> p cb j", p=P)
+                )
+                view_f32[jb, u] = loaded
+
+        w1_sb = held.tile([P, CB, H], BF16, name="w1_sb")
+        nc.scalar.dma_start(w1_sb[:], w1.rearrange("(cb p) h -> p cb h", p=P))
+        load_views(0)
         b1_sb = held.tile([P, 1], F32, name="b1_sb")
         nc.sync.dma_start(b1_sb[:], b1)
         w2_sb = held.tile([P, 1], BF16, name="w2_sb")
-        nc.scalar.dma_start(w2_sb[:], w2)
-        w1_sb = held.tile([P, CB, H], BF16, name="w1_sb")
-        nc.scalar.dma_start(w1_sb[:], w1.rearrange("(cb p) h -> p cb h", p=P))
-        view_f32 = []
-        for u, (view, queue) in enumerate(((xs, nc.sync), (vals, nc.scalar), (xo, nc.sync))):
-            loaded = held.tile([P, CB, N], F32, name=f"view_f32_{u}")
-            queue.dma_start(loaded[:], view.rearrange("(cb p) n -> p cb n", p=P))
-            view_f32.append(loaded)
+        nc.gpsimd.dma_start(w2_sb[:], w2)
+        load_views(1)
         offsets = held.tile([P, N // 16], U16, name="offsets")
         nc.sync.dma_start(offsets[:], offs)
         windows = []
-        for cb, queue in enumerate((nc.sync, nc.scalar)):
+        for cb in range(CB):
             window = held.tile([P, S], F32, name=f"window_{cb}")
-            queue.dma_start(window[:], base_blocks[cb])
+            nc.sync.dma_start(window[:], base_blocks[cb])
             windows.append(window)
 
-        identity = held.tile([P, P], F32, name="identity")
-        make_identity(nc, identity[:])
+        scratch = held.tile([P, 1], F32, name="scratch")
+        nc.vector.memset(scratch[:], 0.0)
+        nc.scalar.activation(scratch[:], scratch[:], ACT.Exp)
+
         ones = held.tile([P, P], F32, name="ones")
         nc.gpsimd.memset(ones[:], 1.0)
+        identity = held.tile([P, P], F32, name="identity")
+        make_identity(nc, identity[:])
 
-        score_ps = psum.tile([P, JB, VIEWS], F32, name="score_ps")
-        for u in range(VIEWS):
-            view_bf = held.tile([P, CB, N], BF16, name=f"view_bf_{u}")
-            nc.vector.tensor_copy(view_bf[:], view_f32[u][:])
-            hid_ps = psum.tile([P, N], F32, name=f"hid_ps_{u}")
-            for cb in range(CB):
-                nc.tensor.matmul(
-                    hid_ps[:], w1_sb[:, cb, :], view_bf[:, cb, :], start=(cb == 0), stop=(cb == CB - 1)
-                )
-            hid_bf = held.tile([P, N], BF16, name=f"hid_bf_{u}")
-            nc.scalar.activation(hid_bf[:], hid_ps[:], ACT.Relu, bias=b1_sb[:, 0:1])
-            for jb in range(JB):
-                nc.tensor.matmul(
-                    score_ps[:, jb, u : u + 1], hid_bf[:, jb * P : (jb + 1) * P], w2_sb[:], start=True, stop=True
-                )
-
-        tanhs = held.tile([P, JB, VIEWS], F32, name="tanhs")
-        nc.scalar.activation(tanhs[:], score_ps[:], ACT.Tanh, scale=0.5)
-        exps = held.tile([P, JB, VIEWS], F32, name="exps")
-        nc.scalar.activation(exps[:], tanhs[:], ACT.Exp, scale=0.5)
-        total = held.tile([P, JB], F32, name="total")
-        nc.vector.tensor_reduce(total[:], exps[:], mybir.AxisListType.X, ALU.add)
-        inverse = held.tile([P, JB], F32, name="inverse")
-        nc.vector.reciprocal(inverse[:], total[:])
-
-        share_cols = held.tile([P, JB, P], F32, name="share_cols")
-        share_ps = psum.tile([P, JB, P], F32, name="share_ps")
+        score_ps = []
         for jb in range(JB):
-            nc.vector.tensor_scalar(
-                share_cols[:, jb, :],
-                ones[:],
-                exps[:, jb, VALS : VALS + 1],
-                inverse[:, jb : jb + 1],
-                ALU.mult,
-                ALU.mult,
-            )
-            nc.tensor.transpose(share_ps[:, jb, :], share_cols[:, jb, :], identity[:])
-        share = held.tile([P, N], F32, name="share")
-        nc.vector.tensor_copy(share[:], share_ps[:].rearrange("p jb j -> p (jb j)"))
+            hid_ps = psum.tile([P, VIEWS, P], F32, name=f"hid_ps_{jb}")
+            for u in range(VIEWS):
+                view_bf = held.tile([P, CB, P], BF16, name=f"view_bf_{jb}_{u}")
+                nc.vector.tensor_copy(view_bf[:], view_f32[jb, u][:])
+                for cb in range(CB):
+                    nc.tensor.matmul(
+                        hid_ps[:, u, :], w1_sb[:, cb, :], view_bf[:, cb, :], start=(cb == 0), stop=(cb == CB - 1)
+                    )
+            hid_bf = held.tile([P, VIEWS, P], BF16, name=f"hid_bf_{jb}")
+            nc.scalar.activation(hid_bf[:], hid_ps[:], ACT.Relu, bias=b1_sb[:])
+            scores = psum.tile([P, VIEWS], F32, name=f"score_ps_{jb}")
+            for u in range(VIEWS):
+                nc.tensor.matmul(scores[:, u : u + 1], hid_bf[:, u, :], w2_sb[:], start=True, stop=True)
+            score_ps.append(scores)
 
-        for cb, queue in enumerate((nc.sync, nc.scalar)):
-            nc.vector.tensor_tensor(
-                windows[cb][:].indirect(offsets[:]), view_f32[VALS][:, cb, :], share[:], ALU.mult
+        share = []
+        for jb in range(JB):
+            tanhs = held.tile([P, VIEWS], F32, name=f"tanhs_{jb}")
+            nc.scalar.activation(tanhs[:], score_ps[jb][:], ACT.Tanh, scale=0.5)
+            exps = held.tile([P, VIEWS], F32, name=f"exps_{jb}")
+            total = held.tile([P, 1], F32, name=f"total_{jb}")
+            nc.scalar.activation(exps[:], tanhs[:], ACT.Exp, scale=0.5, accum_out=total[:])
+            inverse = held.tile([P, 1], F32, name=f"inverse_{jb}")
+            nc.vector.reciprocal(inverse[:], total[:])
+            share_cols = held.tile([P, P], F32, name=f"share_cols_{jb}")
+            nc.vector.tensor_scalar(
+                share_cols[:], ones[:], exps[:, VALS : VALS + 1], inverse[:], ALU.mult, ALU.mult
             )
-            queue.dma_start(out_blocks[cb], windows[cb][:])
+            share_ps = psum.tile([P, P], F32, name=f"share_ps_{jb}")
+            nc.tensor.transpose(share_ps[:], share_cols[:], identity[:])
+            share_rows = held.tile([P, P], F32, name=f"share_rows_{jb}")
+            nc.scalar.copy(share_rows[:], share_ps[:])
+            share.append(share_rows)
+
+        for jb in range(JB):
+            for cb in range(CB):
+                nc.vector.tensor_tensor(
+                    windows[cb][:].indirect(offsets[:, jb * OFFS_COLS : (jb + 1) * OFFS_COLS]),
+                    view_f32[jb, VALS][:, cb, :],
+                    share[jb][:],
+                    ALU.mult,
+                )
+        for cb in range(CB):
+            hw_queues[cb].dma_start(out_blocks[cb], windows[cb][:])

@@ -14,6 +14,7 @@ JB = N // P
 VIEWS = 3
 VALS = 1
 OFFS_COLS = P // 16
+WARM_MATMULS = 8
 
 FLOPS = 2 * C * H * VIEWS * N + 2 * H * VIEWS * N
 
@@ -57,6 +58,12 @@ def tile_attentionnetwork_kernel(tc, base, xs, vals, xo, w1, b1, w2, offs, out):
         scratch = held.tile([P, 1], F32, name="scratch")
         nc.vector.memset(scratch[:], 0.0)
         nc.scalar.activation(scratch[:], scratch[:], ACT.Exp)
+
+        zeros = held.tile([P, 2 * P], BF16, name="zeros")
+        nc.vector.memset(zeros[:], 0.0)
+        warm_ps = psum.tile([P, 2 * P], F32, name="warm_ps")
+        for k in range(WARM_MATMULS):
+            nc.tensor.matmul(warm_ps[:], zeros[:, 0:P], zeros[:], start=True, stop=True)
 
         ones = held.tile([P, P], F32, name="ones")
         nc.gpsimd.memset(ones[:], 1.0)

@@ -1,3 +1,5 @@
+from contextlib import ExitStack
+
 import concourse.mybir as mybir
 from concourse.masks import make_identity
 
@@ -25,10 +27,9 @@ def tile_attentionnetwork_kernel(tc, base, xs, vals, xo, w1, b1, w2, offs, out):
     out_blocks = out.rearrange("(cb p) s -> cb p s", p=P)
     hw_queues = (nc.sync, nc.scalar)
 
-    with (
-        tc.tile_pool(name="held", bufs=1) as held,
-        tc.psum_pool(name="psum", bufs=1) as psum,
-    ):
+    with ExitStack() as ctx:
+        held = ctx.enter_context(tc.tile_pool(name="held", bufs=1))
+
         view_f32 = {}
 
         def load_views(jb):
@@ -61,14 +62,15 @@ def tile_attentionnetwork_kernel(tc, base, xs, vals, xo, w1, b1, w2, offs, out):
 
         zeros = held.tile([P, 2 * P], BF16, name="zeros")
         nc.vector.memset(zeros[:], 0.0)
-        warm_ps = psum.tile([P, 2 * P], F32, name="warm_ps")
-        for k in range(WARM_MATMULS):
-            nc.tensor.matmul(warm_ps[:], zeros[:, 0:P], zeros[:], start=True, stop=True)
+        with tc.psum_pool(name="warm_psum", bufs=1) as warm_psum:
+            warm_ps = warm_psum.tile([P, 2 * P], F32, name="warm_ps")
+            for k in range(WARM_MATMULS):
+                nc.tensor.matmul(warm_ps[:], zeros[:, 0:P], zeros[:], start=True, stop=True)
 
-        ones = held.tile([P, P], F32, name="ones")
-        nc.gpsimd.memset(ones[:], 1.0)
         identity = held.tile([P, P], F32, name="identity")
         make_identity(nc, identity[:])
+
+        psum = ctx.enter_context(tc.psum_pool(name="psum", bufs=1))
 
         score_ps = []
         for jb in range(JB):
@@ -96,14 +98,14 @@ def tile_attentionnetwork_kernel(tc, base, xs, vals, xo, w1, b1, w2, offs, out):
             nc.scalar.activation(exps[:], tanhs[:], ACT.Exp, scale=0.5, accum_out=total[:])
             inverse = held.tile([P, 1], F32, name=f"inverse_{jb}")
             nc.vector.reciprocal(inverse[:], total[:])
-            share_cols = held.tile([P, P], F32, name=f"share_cols_{jb}")
-            nc.vector.tensor_scalar(
-                share_cols[:], ones[:], exps[:, VALS : VALS + 1], inverse[:], ALU.mult, ALU.mult
-            )
-            share_ps = psum.tile([P, P], F32, name=f"share_ps_{jb}")
-            nc.tensor.transpose(share_ps[:], share_cols[:], identity[:])
+            exp_ps = psum.tile([P, P], F32, name=f"exp_ps_{jb}")
+            nc.tensor.transpose(exp_ps[:], exps[:, VALS : VALS + 1].to_broadcast([P, P]), identity[:])
+            exp_rows = held.tile([P, P], F32, name=f"exp_rows_{jb}")
+            nc.scalar.copy(exp_rows[:], exp_ps[:])
+            inverse_ps = psum.tile([P, P], F32, name=f"inverse_ps_{jb}")
+            nc.tensor.transpose(inverse_ps[:], inverse[:].to_broadcast([P, P]), identity[:])
             share_rows = held.tile([P, P], F32, name=f"share_rows_{jb}")
-            nc.scalar.copy(share_rows[:], share_ps[:])
+            nc.vector.tensor_tensor(share_rows[:], inverse_ps[:], exp_rows[:], ALU.mult)
             share.append(share_rows)
 
         for jb in range(JB):

@@ -1,5 +1,3 @@
-from contextlib import ExitStack
-
 import concourse.mybir as mybir
 from concourse.masks import make_identity
 
@@ -27,9 +25,10 @@ def tile_attentionnetwork_kernel(tc, base, xs, vals, xo, w1, b1, w2, offs, out):
     out_blocks = out.rearrange("(cb p) s -> cb p s", p=P)
     hw_queues = (nc.sync, nc.scalar)
 
-    with ExitStack() as ctx:
-        held = ctx.enter_context(tc.tile_pool(name="held", bufs=1))
-
+    with (
+        tc.tile_pool(name="held", bufs=1) as held,
+        tc.psum_pool(name="psum", bufs=1) as psum,
+    ):
         view_f32 = {}
 
         def load_views(jb):
@@ -40,11 +39,11 @@ def tile_attentionnetwork_kernel(tc, base, xs, vals, xo, w1, b1, w2, offs, out):
                 )
                 view_f32[jb, u] = loaded
 
+        b1_sb = held.tile([P, 1], F32, name="b1_sb")
+        nc.sync.dma_start(b1_sb[:], b1)
         w1_sb = held.tile([P, CB, H], BF16, name="w1_sb")
         nc.scalar.dma_start(w1_sb[:], w1.rearrange("(cb p) h -> p cb h", p=P))
         load_views(0)
-        b1_sb = held.tile([P, 1], F32, name="b1_sb")
-        nc.sync.dma_start(b1_sb[:], b1)
         w2_sb = held.tile([P, 1], BF16, name="w2_sb")
         nc.gpsimd.dma_start(w2_sb[:], w2)
         load_views(1)
@@ -62,15 +61,12 @@ def tile_attentionnetwork_kernel(tc, base, xs, vals, xo, w1, b1, w2, offs, out):
 
         zeros = held.tile([P, 2 * P], BF16, name="zeros")
         nc.vector.memset(zeros[:], 0.0)
-        with tc.psum_pool(name="warm_psum", bufs=1) as warm_psum:
-            warm_ps = warm_psum.tile([P, 2 * P], F32, name="warm_ps")
-            for k in range(WARM_MATMULS):
-                nc.tensor.matmul(warm_ps[:], zeros[:, 0:P], zeros[:], start=True, stop=True)
+        warm_ps = psum.tile([P, 2 * P], F32, name="warm_ps")
+        for k in range(WARM_MATMULS):
+            nc.tensor.matmul(warm_ps[:], zeros[:, 0:P], zeros[:], start=True, stop=True)
 
         identity = held.tile([P, P], F32, name="identity")
         make_identity(nc, identity[:])
-
-        psum = ctx.enter_context(tc.psum_pool(name="psum", bufs=1))
 
         score_ps = []
         for jb in range(JB):
@@ -98,14 +94,12 @@ def tile_attentionnetwork_kernel(tc, base, xs, vals, xo, w1, b1, w2, offs, out):
             nc.scalar.activation(exps[:], tanhs[:], ACT.Exp, scale=0.5, accum_out=total[:])
             inverse = held.tile([P, 1], F32, name=f"inverse_{jb}")
             nc.vector.reciprocal(inverse[:], total[:])
-            exp_ps = psum.tile([P, P], F32, name=f"exp_ps_{jb}")
-            nc.tensor.transpose(exp_ps[:], exps[:, VALS : VALS + 1].to_broadcast([P, P]), identity[:])
-            exp_rows = held.tile([P, P], F32, name=f"exp_rows_{jb}")
-            nc.scalar.copy(exp_rows[:], exp_ps[:])
-            inverse_ps = psum.tile([P, P], F32, name=f"inverse_ps_{jb}")
-            nc.tensor.transpose(inverse_ps[:], inverse[:].to_broadcast([P, P]), identity[:])
+            share_col = held.tile([P, 1], F32, name=f"share_col_{jb}")
+            nc.vector.tensor_tensor(share_col[:], exps[:, VALS : VALS + 1], inverse[:], ALU.mult)
+            share_ps = psum.tile([P, P], F32, name=f"share_ps_{jb}")
+            nc.tensor.transpose(share_ps[:], share_col[:].to_broadcast([P, P]), identity[:])
             share_rows = held.tile([P, P], F32, name=f"share_rows_{jb}")
-            nc.vector.tensor_tensor(share_rows[:], inverse_ps[:], exp_rows[:], ALU.mult)
+            nc.scalar.copy(share_rows[:], share_ps[:])
             share.append(share_rows)
 
         for jb in range(JB):

@@ -39,11 +39,11 @@ def tile_attentionnetwork_kernel(tc, base, xs, vals, xo, w1, b1, w2, offs, out):
                 )
                 view_f32[jb, u] = loaded
 
-        b1_sb = held.tile([P, 1], F32, name="b1_sb")
-        nc.sync.dma_start(b1_sb[:], b1)
         w1_sb = held.tile([P, CB, H], BF16, name="w1_sb")
         nc.scalar.dma_start(w1_sb[:], w1.rearrange("(cb p) h -> p cb h", p=P))
         load_views(0)
+        b1_sb = held.tile([P, 1], F32, name="b1_sb")
+        nc.sync.dma_start(b1_sb[:], b1)
         w2_sb = held.tile([P, 1], BF16, name="w2_sb")
         nc.gpsimd.dma_start(w2_sb[:], w2)
         load_views(1)

@@ -70,19 +70,18 @@ def tile_attentionnetwork_kernel(tc, base, xs, vals, xo, w1, b1, w2, offs, out):
 
         score_ps = []
         for jb in range(JB):
-            hid_ps = psum.tile([P, VIEWS, P], F32, name=f"hid_ps_{jb}")
+            scores = psum.tile([P, VIEWS], F32, name=f"score_ps_{jb}")
             for u in range(VIEWS):
                 view_bf = held.tile([P, CB, P], BF16, name=f"view_bf_{jb}_{u}")
                 nc.vector.tensor_copy(view_bf[:], view_f32[jb, u][:])
+                hid_ps = psum.tile([P, P], F32, name=f"hid_ps_{jb}_{u}", tag="hid_ps", bufs=VIEWS)
                 for cb in range(CB):
                     nc.tensor.matmul(
-                        hid_ps[:, u, :], w1_sb[:, cb, :], view_bf[:, cb, :], start=(cb == 0), stop=(cb == CB - 1)
+                        hid_ps[:], w1_sb[:, cb, :], view_bf[:, cb, :], start=(cb == 0), stop=(cb == CB - 1)
                     )
-            hid_bf = held.tile([P, VIEWS, P], BF16, name=f"hid_bf_{jb}")
-            nc.scalar.activation(hid_bf[:], hid_ps[:], ACT.Relu, bias=b1_sb[:])
-            scores = psum.tile([P, VIEWS], F32, name=f"score_ps_{jb}")
-            for u in range(VIEWS):
-                nc.tensor.matmul(scores[:, u : u + 1], hid_bf[:, u, :], w2_sb[:], start=True, stop=True)
+                hid_bf = held.tile([P, P], BF16, name=f"hid_bf_{jb}_{u}")
+                nc.scalar.activation(hid_bf[:], hid_ps[:], ACT.Relu, bias=b1_sb[:])
+                nc.tensor.matmul(scores[:, u : u + 1], hid_bf[:], w2_sb[:], start=True, stop=True)
             score_ps.append(scores)
 
         share = []

@@ -14,6 +14,7 @@ JB = N // P
 VIEWS = 3
 VALS = 1
 OFFS_COLS = P // 16
+HW_DMAS_IN_FLIGHT = 8
 WARM_MATMULS = 8
 
 FLOPS = 2 * C * H * VIEWS * N + 2 * H * VIEWS * N
@@ -29,24 +30,31 @@ def tile_attentionnetwork_kernel(tc, base, xs, vals, xo, w1, b1, w2, offs, out):
         tc.tile_pool(name="held", bufs=1) as held,
         tc.psum_pool(name="psum", bufs=1) as psum,
     ):
+        loads_issued = []
+
+        def load(tile_ap, source):
+            queue = hw_queues[len(loads_issued) % 2] if len(loads_issued) < HW_DMAS_IN_FLIGHT else nc.sync
+            queue.dma_start(tile_ap, source)
+            loads_issued.append(queue)
+
         view_f32 = {}
 
-        def load_views(jb):
-            for u, view in enumerate((xs, vals, xo)):
-                loaded = held.tile([P, CB, P], F32, name=f"view_f32_{jb}_{u}")
-                hw_queues[(jb * VIEWS + u) % 2].dma_start(
-                    loaded[:], view[:, jb * P : (jb + 1) * P].rearrange("(cb p) j -> p cb j", p=P)
-                )
-                view_f32[jb, u] = loaded
+        def load_view(jb, u):
+            loaded = held.tile([P, CB, P], F32, name=f"view_f32_{jb}_{u}")
+            load(loaded[:], (xs, vals, xo)[u][:, jb * P : (jb + 1) * P].rearrange("(cb p) j -> p cb j", p=P))
+            view_f32[jb, u] = loaded
 
+        load_view(0, 0)
         w1_sb = held.tile([P, CB, H], BF16, name="w1_sb")
-        nc.scalar.dma_start(w1_sb[:], w1.rearrange("(cb p) h -> p cb h", p=P))
-        load_views(0)
+        load(w1_sb[:], w1.rearrange("(cb p) h -> p cb h", p=P))
+        load_view(0, 1)
+        load_view(0, 2)
         b1_sb = held.tile([P, 1], F32, name="b1_sb")
-        nc.sync.dma_start(b1_sb[:], b1)
+        load(b1_sb[:], b1)
         w2_sb = held.tile([P, 1], BF16, name="w2_sb")
-        nc.gpsimd.dma_start(w2_sb[:], w2)
-        load_views(1)
+        load(w2_sb[:], w2)
+        for u in range(VIEWS):
+            load_view(1, u)
         offsets = held.tile([P, N // 16], U16, name="offsets")
         nc.sync.dma_start(offsets[:], offs)
         windows = []

@@ -12,7 +12,7 @@ C, H, S, N = 256, 128, 512, 256
 CB = C // P
 JB = N // P
 VIEWS = 3
-VALS = 1
+VALS = 0
 OFFS_COLS = P // 16
 HW_DMAS_IN_FLIGHT = 8
 WARM_MATMULS = 8
@@ -22,8 +22,8 @@ FLOPS = 2 * C * H * VIEWS * N + 2 * H * VIEWS * N
 
 def tile_attentionnetwork_kernel(tc, base, xs, vals, xo, w1, b1, w2, offs, out):
     nc = tc.nc
-    base_blocks = base.rearrange("(cb p) s -> cb p s", p=P)
-    out_blocks = out.rearrange("(cb p) s -> cb p s", p=P)
+    base_blocks = base.rearrange("(p cb) s -> cb p s", cb=CB)
+    out_blocks = out.rearrange("(p cb) s -> cb p s", cb=CB)
     hw_queues = (nc.sync, nc.scalar)
 
     with (
@@ -41,16 +41,16 @@ def tile_attentionnetwork_kernel(tc, base, xs, vals, xo, w1, b1, w2, offs, out):
 
         def load_view(jb, u):
             loaded = held.tile([P, CB, P], F32, name=f"view_f32_{jb}_{u}")
-            load(loaded[:], (xs, vals, xo)[u][:, jb * P : (jb + 1) * P].rearrange("(cb p) j -> p cb j", p=P))
+            load(loaded[:], (vals, xs, xo)[u][:, jb * P : (jb + 1) * P].rearrange("(p cb) j -> p cb j", cb=CB))
             view_f32[jb, u] = loaded
 
         load_view(0, 0)
         w1_sb = held.tile([P, CB, H], BF16, name="w1_sb")
-        load(w1_sb[:], w1.rearrange("(cb p) h -> p cb h", p=P))
+        load(w1_sb[:], w1.rearrange("(p cb) h -> p cb h", cb=CB))
         load_view(0, 1)
-        load_view(0, 2)
         b1_sb = held.tile([P, 1], F32, name="b1_sb")
         load(b1_sb[:], b1)
+        load_view(0, 2)
         w2_sb = held.tile([P, 1], BF16, name="w2_sb")
         load(w2_sb[:], w2)
         for u in range(VIEWS):
@@ -77,8 +77,11 @@ def tile_attentionnetwork_kernel(tc, base, xs, vals, xo, w1, b1, w2, offs, out):
         make_identity(nc, identity[:])
 
         score_ps = []
+        tanhs, shifts = [], []
         for jb in range(JB):
             scores = psum.tile([P, VIEWS], F32, name=f"score_ps_{jb}")
+            block_tanhs = held.tile([P, VIEWS], F32, name=f"tanhs_{jb}")
+            shift = held.tile([P, 1], F32, name=f"shift_{jb}")
             for u in range(VIEWS):
                 view_bf = held.tile([P, CB, P], BF16, name=f"view_bf_{jb}_{u}")
                 nc.vector.tensor_copy(view_bf[:], view_f32[jb, u][:])
@@ -90,19 +93,24 @@ def tile_attentionnetwork_kernel(tc, base, xs, vals, xo, w1, b1, w2, offs, out):
                 hid_bf = held.tile([P, P], BF16, name=f"hid_bf_{jb}_{u}")
                 nc.scalar.activation(hid_bf[:], hid_ps[:], ACT.Relu, bias=b1_sb[:])
                 nc.tensor.matmul(scores[:, u : u + 1], hid_bf[:], w2_sb[:], start=True, stop=True)
+                if u == VALS:
+                    nc.scalar.activation(block_tanhs[:, u : u + 1], scores[:, u : u + 1], ACT.Tanh, scale=0.5)
+                    nc.vector.tensor_scalar_mul(shift[:], block_tanhs[:, u : u + 1], -0.5)
             score_ps.append(scores)
+            tanhs.append(block_tanhs)
+            shifts.append(shift)
 
         share = []
         for jb in range(JB):
-            tanhs = held.tile([P, VIEWS], F32, name=f"tanhs_{jb}")
-            nc.scalar.activation(tanhs[:], score_ps[jb][:], ACT.Tanh, scale=0.5)
+            others = slice(VALS + 1, VIEWS)
+            nc.scalar.activation(tanhs[jb][:, others], score_ps[jb][:, others], ACT.Tanh, scale=0.5)
             exps = held.tile([P, VIEWS], F32, name=f"exps_{jb}")
             total = held.tile([P, 1], F32, name=f"total_{jb}")
-            nc.scalar.activation(exps[:], tanhs[:], ACT.Exp, scale=0.5, accum_out=total[:])
-            inverse = held.tile([P, 1], F32, name=f"inverse_{jb}")
-            nc.vector.reciprocal(inverse[:], total[:])
+            nc.scalar.activation(
+                exps[:], tanhs[jb][:], ACT.Exp, bias=shifts[jb][:], scale=0.5, accum_out=total[:]
+            )
             share_col = held.tile([P, 1], F32, name=f"share_col_{jb}")
-            nc.vector.tensor_tensor(share_col[:], exps[:, VALS : VALS + 1], inverse[:], ALU.mult)
+            nc.vector.reciprocal(share_col[:], total[:])
             share_ps = psum.tile([P, P], F32, name=f"share_ps_{jb}")
             nc.tensor.transpose(share_ps[:], share_col[:].to_broadcast([P, P]), identity[:])
             share_rows = held.tile([P, P], F32, name=f"share_rows_{jb}")

@@ -91,7 +91,10 @@ def tile_attentionnetwork_kernel(tc, base, xs, vals, xo, w1, b1, w2, offs, out):
                         hid_ps[:], w1_sb[:, cb, :], view_bf[:, cb, :], start=(cb == 0), stop=(cb == CB - 1)
                     )
                 hid_bf = held.tile([P, P], BF16, name=f"hid_bf_{jb}_{u}")
-                nc.scalar.activation(hid_bf[:], hid_ps[:], ACT.Relu, bias=b1_sb[:])
+                if jb == 0:
+                    nc.scalar.activation(hid_bf[:], hid_ps[:], ACT.Relu, bias=b1_sb[:])
+                else:
+                    nc.vector.tensor_scalar(hid_bf[:], hid_ps[:], b1_sb[:], 0.0, ALU.add, ALU.max)
                 nc.tensor.matmul(scores[:, u : u + 1], hid_bf[:], w2_sb[:], start=True, stop=True)
                 if u == VALS:
                     nc.scalar.activation(block_tanhs[:, u : u + 1], scores[:, u : u + 1], ACT.Tanh, scale=0.5)

@@ -48,9 +48,9 @@ def tile_attentionnetwork_kernel(tc, base, xs, vals, xo, w1, b1, w2, offs, out):
         w1_sb = held.tile([P, CB, H], BF16, name="w1_sb")
         load(w1_sb[:], w1.rearrange("(p cb) h -> p cb h", cb=CB))
         load_view(0, 1)
+        load_view(0, 2)
         b1_sb = held.tile([P, 1], F32, name="b1_sb")
         load(b1_sb[:], b1)
-        load_view(0, 2)
         w2_sb = held.tile([P, 1], BF16, name="w2_sb")
         load(w2_sb[:], w2)
         for u in range(VIEWS):

@@ -68,7 +68,7 @@ def tile_attentionnetwork_kernel(tc, base, xs, vals, xo, w1, b1, w2, offs, out):
         nc.scalar.activation(scratch[:], scratch[:], ACT.Exp)
 
         zeros = held.tile([P, 2 * P], BF16, name="zeros")
-        nc.vector.memset(zeros[:], 0.0)
+        nc.gpsimd.memset(zeros[:], 0.0)
         warm_ps = psum.tile([P, 2 * P], F32, name="warm_ps")
         for k in range(WARM_MATMULS):
             nc.tensor.matmul(warm_ps[:], zeros[:, 0:P], zeros[:], start=True, stop=True)

@@ -12,9 +12,8 @@ C, H, S, N = 256, 128, 512, 256
 CB = C // P
 JB = N // P
 VIEWS = 3
-VALS = 0
+VALS, XS, XO = range(VIEWS)
 OFFS_COLS = P // 16
-HW_DMAS_IN_FLIGHT = 8
 WARM_MATMULS = 8
 
 FLOPS = 2 * C * H * VIEWS * N + 2 * H * VIEWS * N
@@ -30,31 +29,26 @@ def tile_attentionnetwork_kernel(tc, base, xs, vals, xo, w1, b1, w2, offs, out):
         tc.tile_pool(name="held", bufs=1) as held,
         tc.psum_pool(name="psum", bufs=1) as psum,
     ):
-        loads_issued = []
-
-        def load(tile_ap, source):
-            queue = hw_queues[len(loads_issued) % 2] if len(loads_issued) < HW_DMAS_IN_FLIGHT else nc.sync
-            queue.dma_start(tile_ap, source)
-            loads_issued.append(queue)
-
         view_f32 = {}
 
-        def load_view(jb, u):
+        def load_view(queue, jb, u):
             loaded = held.tile([P, CB, P], F32, name=f"view_f32_{jb}_{u}")
-            load(loaded[:], (vals, xs, xo)[u][:, jb * P : (jb + 1) * P].rearrange("(p cb) j -> p cb j", cb=CB))
+            source = (vals, xs, xo)[u][:, jb * P : (jb + 1) * P]
+            queue.dma_start(loaded[:], source.rearrange("(p cb) j -> p cb j", cb=CB))
             view_f32[jb, u] = loaded
 
-        load_view(0, 0)
+        load_view(nc.sync, 0, VALS)
         w1_sb = held.tile([P, CB, H], BF16, name="w1_sb")
-        load(w1_sb[:], w1.rearrange("(p cb) h -> p cb h", cb=CB))
-        load_view(0, 1)
-        load_view(0, 2)
+        nc.scalar.dma_start(w1_sb[:], w1.rearrange("(p cb) h -> p cb h", cb=CB))
+        load_view(nc.scalar, 0, XS)
+        load_view(nc.sync, 0, XO)
         b1_sb = held.tile([P, 1], F32, name="b1_sb")
-        load(b1_sb[:], b1)
+        nc.sync.dma_start(b1_sb[:], b1)
         w2_sb = held.tile([P, 1], BF16, name="w2_sb")
-        load(w2_sb[:], w2)
-        for u in range(VIEWS):
-            load_view(1, u)
+        nc.scalar.dma_start(w2_sb[:], w2)
+        load_view(nc.sync, 1, VALS)
+        load_view(nc.scalar, 1, XS)
+        load_view(nc.sync, 1, XO)
         offsets = held.tile([P, N // 16], U16, name="offsets")
         nc.sync.dma_start(offsets[:], offs)
         windows = []

@@ -37,15 +37,15 @@ def tile_attentionnetwork_kernel(tc, base, xs, vals, xo, w1, b1, w2, offs, out):
             queue.dma_start(loaded[:], source.rearrange("(p cb) j -> p cb j", cb=CB))
             view_f32[jb, u] = loaded
 
+        b1_row = held.tile([1, H], F32, name="b1_row")
+        nc.scalar.dma_start(b1_row[:], b1.rearrange("h o -> o h"))
+        w2_row = held.tile([1, H], BF16, name="w2_row")
+        nc.sync.dma_start(w2_row[:], w2.rearrange("h o -> o h"))
         load_view(nc.sync, 0, VALS)
         w1_sb = held.tile([P, CB, H], BF16, name="w1_sb")
         nc.scalar.dma_start(w1_sb[:], w1.rearrange("(p cb) h -> p cb h", cb=CB))
         load_view(nc.scalar, 0, XS)
         load_view(nc.sync, 0, XO)
-        b1_sb = held.tile([P, 1], F32, name="b1_sb")
-        nc.sync.dma_start(b1_sb[:], b1)
-        w2_sb = held.tile([P, 1], BF16, name="w2_sb")
-        nc.scalar.dma_start(w2_sb[:], w2)
         load_view(nc.sync, 1, VALS)
         load_view(nc.scalar, 1, XS)
         load_view(nc.sync, 1, XO)
@@ -69,6 +69,18 @@ def tile_attentionnetwork_kernel(tc, base, xs, vals, xo, w1, b1, w2, offs, out):
 
         identity = held.tile([P, P], F32, name="identity")
         make_identity(nc, identity[:])
+
+        def column(row, dtype, name):
+            one = held.tile([1, 1], dtype, name=f"{name}_one")
+            nc.vector.memset(one[:], 1.0)
+            column_ps = psum.tile([P, 1], F32, name=f"{name}_ps", tag="hid_ps", bufs=VIEWS)
+            nc.tensor.matmul(column_ps[:], row[:], one[:], start=True, stop=True)
+            turned = held.tile([P, 1], dtype, name=name)
+            nc.vector.tensor_copy(turned[:], column_ps[:])
+            return turned
+
+        b1_sb = column(b1_row, F32, "b1_sb")
+        w2_sb = column(w2_row, BF16, "w2_sb")
 
         score_ps = []
         tanhs, shifts = [], []

@@ -14,7 +14,7 @@ JB = N // P
 VIEWS = 3
 VALS, XS, XO = range(VIEWS)
 OFFS_COLS = P // 16
-WARM_MATMULS = 8
+WARM_MATMULS = 6
 
 FLOPS = 2 * C * H * VIEWS * N + 2 * H * VIEWS * N
 
@@ -76,7 +76,7 @@ def tile_attentionnetwork_kernel(tc, base, xs, vals, xo, w1, b1, w2, offs, out):
             column_ps = psum.tile([P, 1], F32, name=f"{name}_ps", tag="hid_ps", bufs=VIEWS)
             nc.tensor.matmul(column_ps[:], row[:], one[:], start=True, stop=True)
             turned = held.tile([P, 1], dtype, name=name)
-            nc.vector.tensor_copy(turned[:], column_ps[:])
+            nc.scalar.copy(turned[:], column_ps[:])
             return turned
 
         b1_sb = column(b1_row, F32, "b1_sb")

@@ -63,7 +63,7 @@ def tile_attentionnetwork_kernel(tc, base, xs, vals, xo, w1, b1, w2, offs, out):
 
         zeros = held.tile([P, 2 * P], BF16, name="zeros")
         nc.gpsimd.memset(zeros[:], 0.0)
-        warm_ps = psum.tile([P, 2 * P], F32, name="warm_ps")
+        warm_ps = psum.tile([P, 2 * P], F32, name="warm_ps", tag="hid_ps", bufs=VIEWS)
         for k in range(WARM_MATMULS):
             nc.tensor.matmul(warm_ps[:], zeros[:, 0:P], zeros[:], start=True, stop=True)
 
@@ -82,11 +82,11 @@ def tile_attentionnetwork_kernel(tc, base, xs, vals, xo, w1, b1, w2, offs, out):
         b1_sb = column(b1_row, F32, "b1_sb")
         w2_sb = column(w2_row, BF16, "w2_sb")
 
-        score_ps = []
-        tanhs, shifts = [], []
-        for jb in range(JB):
-            scores = psum.tile([P, VIEWS], F32, name=f"score_ps_{jb}")
-            block_tanhs = held.tile([P, VIEWS], F32, name=f"tanhs_{jb}")
+        vals_scores = psum.tile([P, JB], F32, name="vals_scores")
+
+        def score_views(jb):
+            other_scores = psum.tile([P, VIEWS - 1], F32, name=f"other_scores_{jb}")
+            tanhs = held.tile([P, VIEWS], F32, name=f"tanhs_{jb}")
             shift = held.tile([P, 1], F32, name=f"shift_{jb}")
             for u in range(VIEWS):
                 view_bf = held.tile([P, CB, P], BF16, name=f"view_bf_{jb}_{u}")
@@ -101,38 +101,42 @@ def tile_attentionnetwork_kernel(tc, base, xs, vals, xo, w1, b1, w2, offs, out):
                     nc.scalar.activation(hid_bf[:], hid_ps[:], ACT.Relu, bias=b1_sb[:])
                 else:
                     nc.vector.tensor_scalar(hid_bf[:], hid_ps[:], b1_sb[:], 0.0, ALU.add, ALU.max)
-                nc.tensor.matmul(scores[:, u : u + 1], hid_bf[:], w2_sb[:], start=True, stop=True)
+                score = vals_scores[:, jb : jb + 1] if u == VALS else other_scores[:, u - 1 : u]
+                nc.tensor.matmul(score, hid_bf[:], w2_sb[:], start=True, stop=True)
                 if u == VALS:
-                    nc.scalar.activation(block_tanhs[:, u : u + 1], scores[:, u : u + 1], ACT.Tanh, scale=0.5)
-                    nc.vector.tensor_scalar_mul(shift[:], block_tanhs[:, u : u + 1], -0.5)
-            score_ps.append(scores)
-            tanhs.append(block_tanhs)
-            shifts.append(shift)
+                    nc.scalar.activation(tanhs[:, u : u + 1], score, ACT.Tanh, scale=0.5)
+                    nc.scalar.mul(shift[:], tanhs[:, u : u + 1], -0.5)
+            return other_scores, tanhs, shift
 
-        share = []
-        for jb in range(JB):
-            others = slice(VALS + 1, VIEWS)
-            nc.scalar.activation(tanhs[jb][:, others], score_ps[jb][:, others], ACT.Tanh, scale=0.5)
+        def share_of_vals(jb, other_scores, tanhs, shift):
+            nc.scalar.activation(tanhs[:, VALS + 1 :], other_scores[:], ACT.Tanh, scale=0.5)
             exps = held.tile([P, VIEWS], F32, name=f"exps_{jb}")
             total = held.tile([P, 1], F32, name=f"total_{jb}")
-            nc.scalar.activation(
-                exps[:], tanhs[jb][:], ACT.Exp, bias=shifts[jb][:], scale=0.5, accum_out=total[:]
-            )
+            nc.scalar.activation(exps[:], tanhs[:], ACT.Exp, bias=shift[:], scale=0.5, accum_out=total[:])
             share_col = held.tile([P, 1], F32, name=f"share_col_{jb}")
             nc.vector.reciprocal(share_col[:], total[:])
             share_ps = psum.tile([P, P], F32, name=f"share_ps_{jb}")
             nc.tensor.transpose(share_ps[:], share_col[:].to_broadcast([P, P]), identity[:])
             share_rows = held.tile([P, P], F32, name=f"share_rows_{jb}")
             nc.scalar.copy(share_rows[:], share_ps[:])
-            share.append(share_rows)
+            return share_rows
 
-        for jb in range(JB):
-            for cb in range(CB):
-                nc.vector.tensor_tensor(
-                    windows[cb][:].indirect(offsets[:, jb * OFFS_COLS : (jb + 1) * OFFS_COLS]),
-                    view_f32[jb, VALS][:, cb, :],
-                    share[jb][:],
-                    ALU.mult,
-                )
+        def place(jb, cb, share_rows):
+            nc.vector.tensor_tensor(
+                windows[cb][:].indirect(offsets[:, jb * OFFS_COLS : (jb + 1) * OFFS_COLS]),
+                view_f32[jb, VALS][:, cb, :],
+                share_rows[:],
+                ALU.mult,
+            )
+
+        gate_0 = score_views(0)
+        gate_1 = score_views(1)
+        share_0 = share_of_vals(0, *gate_0)
+        share_1 = share_of_vals(1, *gate_1)
+        place(0, 0, share_0)
+        place(0, 1, share_0)
+        place(1, 0, share_1)
+        place(1, 1, share_1)
+
         for cb in range(CB):
             hw_queues[cb].dma_start(out_blocks[cb], windows[cb][:])

@@ -23,7 +23,6 @@ def tile_attentionnetwork_kernel(tc, base, xs, vals, xo, w1, b1, w2, offs, out):
     nc = tc.nc
     base_blocks = base.rearrange("(p cb) s -> cb p s", cb=CB)
     out_blocks = out.rearrange("(p cb) s -> cb p s", cb=CB)
-    hw_queues = (nc.sync, nc.scalar)
 
     with (
         tc.tile_pool(name="held", bufs=1) as held,
@@ -90,7 +89,10 @@ def tile_attentionnetwork_kernel(tc, base, xs, vals, xo, w1, b1, w2, offs, out):
             shift = held.tile([P, 1], F32, name=f"shift_{jb}")
             for u in range(VIEWS):
                 view_bf = held.tile([P, CB, P], BF16, name=f"view_bf_{jb}_{u}")
-                nc.vector.tensor_copy(view_bf[:], view_f32[jb, u][:])
+                halves = CB if (jb, u) == (0, XO) else 1
+                for h in range(halves):
+                    part = slice(h * CB // halves, (h + 1) * CB // halves)
+                    nc.vector.tensor_copy(view_bf[:, part, :], view_f32[jb, u][:, part, :])
                 hid_ps = psum.tile([P, P], F32, name=f"hid_ps_{jb}_{u}", tag="hid_ps", bufs=VIEWS)
                 for cb in range(CB):
                     nc.tensor.matmul(
@@ -138,5 +140,5 @@ def tile_attentionnetwork_kernel(tc, base, xs, vals, xo, w1, b1, w2, offs, out):
         place(1, 0, share_1)
         place(1, 1, share_1)
 
-        for cb in range(CB):
-            hw_queues[cb].dma_start(out_blocks[cb], windows[cb][:])
+        nc.scalar.dma_start(out_blocks[0], windows[0][:])
+        nc.sync.dma_start(out_blocks[1], windows[1][:])

import concourse.mybir as mybir
from concourse.masks import make_identity

F32 = mybir.dt.float32
BF16 = mybir.dt.bfloat16
U16 = mybir.dt.uint16
ALU = mybir.AluOpType
ACT = mybir.ActivationFunctionType

P = 128
C, H, S, N = 256, 128, 512, 256
CB = C // P
JB = N // P
VIEWS = 3
VALS, XS, XO = range(VIEWS)
OFFS_COLS = P // 16
WARM_MATMULS = 6

FLOPS = 2 * C * H * VIEWS * N + 2 * H * VIEWS * N


def tile_attentionnetwork_kernel(tc, base, xs, vals, xo, w1, b1, w2, offs, out):
    nc = tc.nc
    base_blocks = base.rearrange("(p cb) s -> cb p s", cb=CB)
    out_blocks = out.rearrange("(p cb) s -> cb p s", cb=CB)

    with (
        tc.tile_pool(name="held", bufs=1) as held,
        tc.psum_pool(name="psum", bufs=1) as psum,
    ):
        view_f32 = {}

        def load_view(queue, jb, u):
            loaded = held.tile([P, CB, P], F32, name=f"view_f32_{jb}_{u}")
            source = (vals, xs, xo)[u][:, jb * P : (jb + 1) * P]
            queue.dma_start(loaded[:], source.rearrange("(p cb) j -> p cb j", cb=CB))
            view_f32[jb, u] = loaded

        b1_row = held.tile([1, H], F32, name="b1_row")
        nc.scalar.dma_start(b1_row[:], b1.rearrange("h o -> o h"))
        w2_row = held.tile([1, H], BF16, name="w2_row")
        nc.sync.dma_start(w2_row[:], w2.rearrange("h o -> o h"))
        load_view(nc.sync, 0, VALS)
        w1_sb = held.tile([P, CB, H], BF16, name="w1_sb")
        nc.scalar.dma_start(w1_sb[:], w1.rearrange("(p cb) h -> p cb h", cb=CB))
        load_view(nc.scalar, 0, XS)
        load_view(nc.sync, 0, XO)
        load_view(nc.sync, 1, VALS)
        load_view(nc.scalar, 1, XS)
        load_view(nc.sync, 1, XO)
        offsets = held.tile([P, N // 16], U16, name="offsets")
        nc.sync.dma_start(offsets[:], offs)
        windows = []
        for cb in range(CB):
            window = held.tile([P, S], F32, name=f"window_{cb}")
            nc.sync.dma_start(window[:], base_blocks[cb])
            windows.append(window)

        scratch = held.tile([P, 1], F32, name="scratch")
        nc.vector.memset(scratch[:], 0.0)
        nc.scalar.activation(scratch[:], scratch[:], ACT.Exp)

        zeros = held.tile([P, 2 * P], BF16, name="zeros")
        nc.gpsimd.memset(zeros[:], 0.0)
        warm_ps = psum.tile([P, 2 * P], F32, name="warm_ps", tag="hid_ps", bufs=VIEWS)
        for k in range(WARM_MATMULS):
            nc.tensor.matmul(warm_ps[:], zeros[:, 0:P], zeros[:], start=True, stop=True)

        identity = held.tile([P, P], F32, name="identity")
        make_identity(nc, identity[:])

        def column(row, dtype, name):
            one = held.tile([1, 1], dtype, name=f"{name}_one")
            nc.vector.memset(one[:], 1.0)
            column_ps = psum.tile([P, 1], F32, name=f"{name}_ps", tag="hid_ps", bufs=VIEWS)
            nc.tensor.matmul(column_ps[:], row[:], one[:], start=True, stop=True)
            turned = held.tile([P, 1], dtype, name=name)
            nc.scalar.copy(turned[:], column_ps[:])
            return turned

        b1_sb = column(b1_row, F32, "b1_sb")
        w2_sb = column(w2_row, BF16, "w2_sb")

        vals_scores = psum.tile([P, JB], F32, name="vals_scores")

        def score_views(jb):
            other_scores = psum.tile([P, VIEWS - 1], F32, name=f"other_scores_{jb}")
            tanhs = held.tile([P, VIEWS], F32, name=f"tanhs_{jb}")
            shift = held.tile([P, 1], F32, name=f"shift_{jb}")
            for u in range(VIEWS):
                view_bf = held.tile([P, CB, P], BF16, name=f"view_bf_{jb}_{u}")
                halves = CB if (jb, u) == (0, XO) else 1
                for h in range(halves):
                    part = slice(h * CB // halves, (h + 1) * CB // halves)
                    nc.vector.tensor_copy(view_bf[:, part, :], view_f32[jb, u][:, part, :])
                hid_ps = psum.tile([P, P], F32, name=f"hid_ps_{jb}_{u}", tag="hid_ps", bufs=VIEWS)
                for cb in range(CB):
                    nc.tensor.matmul(
                        hid_ps[:], w1_sb[:, cb, :], view_bf[:, cb, :], start=(cb == 0), stop=(cb == CB - 1)
                    )
                hid_bf = held.tile([P, P], BF16, name=f"hid_bf_{jb}_{u}")
                if jb == 0:
                    nc.scalar.activation(hid_bf[:], hid_ps[:], ACT.Relu, bias=b1_sb[:])
                else:
                    nc.vector.tensor_scalar(hid_bf[:], hid_ps[:], b1_sb[:], 0.0, ALU.add, ALU.max)
                score = vals_scores[:, jb : jb + 1] if u == VALS else other_scores[:, u - 1 : u]
                nc.tensor.matmul(score, hid_bf[:], w2_sb[:], start=True, stop=True)
                if u == VALS:
                    nc.scalar.activation(tanhs[:, u : u + 1], score, ACT.Tanh, scale=0.5)
                    nc.scalar.mul(shift[:], tanhs[:, u : u + 1], -0.5)
            return other_scores, tanhs, shift

        def share_of_vals(jb, other_scores, tanhs, shift):
            nc.scalar.activation(tanhs[:, VALS + 1 :], other_scores[:], ACT.Tanh, scale=0.5)
            exps = held.tile([P, VIEWS], F32, name=f"exps_{jb}")
            total = held.tile([P, 1], F32, name=f"total_{jb}")
            nc.scalar.activation(exps[:], tanhs[:], ACT.Exp, bias=shift[:], scale=0.5, accum_out=total[:])
            share_col = held.tile([P, 1], F32, name=f"share_col_{jb}")
            nc.vector.reciprocal(share_col[:], total[:])
            share_ps = psum.tile([P, P], F32, name=f"share_ps_{jb}")
            nc.tensor.transpose(share_ps[:], share_col[:].to_broadcast([P, P]), identity[:])
            share_rows = held.tile([P, P], F32, name=f"share_rows_{jb}")
            nc.scalar.copy(share_rows[:], share_ps[:])
            return share_rows

        def place(jb, cb, share_rows):
            nc.vector.tensor_tensor(
                windows[cb][:].indirect(offsets[:, jb * OFFS_COLS : (jb + 1) * OFFS_COLS]),
                view_f32[jb, VALS][:, cb, :],
                share_rows[:],
                ALU.mult,
            )

        gate_0 = score_views(0)
        gate_1 = score_views(1)
        share_0 = share_of_vals(0, *gate_0)
        share_1 = share_of_vals(1, *gate_1)
        place(0, 0, share_0)
        place(0, 1, share_0)
        place(1, 0, share_1)
        place(1, 1, share_1)

        nc.scalar.dma_start(out_blocks[0], windows[0][:])
        nc.sync.dma_start(out_blocks[1], windows[1][:])
